import numpy as np
import ml_dtypes


def mxq(x, axis, fmt="e4m3"):
    dtype, down = {"e4m3": (ml_dtypes.float8_e4m3fn, 7), "e5m2": (ml_dtypes.float8_e5m2, 14)}[fmt]
    v = np.moveaxis(np.asarray(x, np.float32).astype(ml_dtypes.bfloat16).astype(np.float64), axis, -1)
    blocks = v.reshape(v.shape[:-1] + (-1, 32))
    amax = np.abs(blocks).max(-1, keepdims=True)
    byte = np.maximum(np.where(amax > 0, np.frexp(amax)[1] - 1 + 127, 0) - down, 1)
    scale = np.exp2(byte - 127.0)
    codes = (blocks / scale).astype(np.float32).astype(dtype).astype(np.float64)
    return np.moveaxis((codes * scale).reshape(v.shape), -1, axis)


WIDE = False


def mx_kscale(k):
    if not WIDE:
        return np.ones(k)
    levels = np.array([10, -10, 5, -5, 0])
    if k % 512:
        return np.exp2(np.random.permutation(np.resize(levels, k // 32))).repeat(32)
    a = np.empty((k // 512, 16))
    for p in range(k // 512):
        a[p, :8] = np.random.permutation(np.resize(levels, 8))
        for g in range(8):
            far = levels[np.abs(levels - a[p, g]) >= 10]
            a[p, g + 8] = far[np.random.randint(len(far))]
    return np.exp2(a.ravel()).repeat(32)


BF16 = ml_dtypes.bfloat16


def bf(x):
    return np.asarray(x, np.float32).astype(BF16)


def f64(x):
    return np.asarray(x).astype(np.float64)


B, I, H = 8192, 1024, 128
MXH = H % 512 == 0


def sigmoid(v):
    return 1.0 / (1.0 + np.exp(-v))


def setup_inputs():
    s = mx_kscale(I)
    t = mx_kscale(H) if MXH else np.ones(H)
    return {"x": bf(np.random.standard_normal((B, I)) * s),
            "h": bf(np.random.standard_normal((B, H)) * t),
            "c": bf(np.random.standard_normal((B, H))),
            "Wx": bf(np.random.standard_normal((4, H, I)) * 0.8 / np.sqrt(I) / s),
            "Wh": bf(np.random.standard_normal((4, H, H)) * 0.8 / np.sqrt(H) / t),
            "bx": bf(np.random.standard_normal((4, H)) * 0.3),
            "bh": bf(np.random.standard_normal((4, H)) * 0.3)}


def reference(x, h, c, Wx, Wh, bx, bh):
    wx = f64(Wx).reshape(4 * H, I)
    wh = f64(Wh).reshape(4 * H, H)
    gx = (mxq(f64(x), 1, "e4m3") @ mxq(wx, 1, "e4m3").T) + f64(bx).reshape(-1)
    if MXH:
        gh = (mxq(f64(h), 1, "e4m3") @ mxq(wh, 1, "e4m3").T) + f64(bh).reshape(-1)
    else:
        gh = f64(h) @ wh.T + f64(bh).reshape(-1)
    g = (gx + gh).reshape(-1, 4, H)
    i = sigmoid(g[:, 0])
    f = sigmoid(g[:, 1])
    gc = np.tanh(g[:, 2])
    o = sigmoid(g[:, 3])
    c_new = f * f64(c) + i * gc
    hs = o * np.tanh(c_new)
    return (hs, c_new)

@@ -1,0 +1,443 @@
+from contextlib import ExitStack
+
+import concourse.mybir as mybir
+from concourse.masks import make_identity
+
+F32 = mybir.dt.float32
+BF16 = mybir.dt.bfloat16
+U32 = mybir.dt.uint32
+U8 = mybir.dt.uint8
+FP8X4 = mybir.dt.float8_e4m3fn_x4
+AF = mybir.ActivationFunctionType
+ALU = mybir.AluOpType
+
+P = 128
+B, I, H = 8192, 1024, 128
+NT = B // P
+NPAIR = NT // 2
+NQUAD = NT // 4
+G4 = 4 * H
+FLOPS = 2 * B * (I + H) * G4
+POS = (0, 1, 3, 2)
+INV = (0, 1, 3, 2)
+
+PIN = True
+XT_BUFS = 4
+GX_BUFS = 2
+GHA_BUFS = 0
+LOOK = 3
+OFF = 3
+NTAILQ = 2
+C_EVERY = 2
+C_PHASE = 1
+GRP_BUFS = 3
+GQ_BUFS = 6
+T2_BUFS = 1
+T1_BUFS = 1
+CP1 = "s"
+TAIL_S = 1
+
+
+HEAD_RAMP = 1
+QWHOLE = 2
+LASTW = NQUAD - 3
+XCE = "ss"
+XCO = "sv"
+CP0 = "s"
+CP0B = "v"
+CP1B = "s"
+HTE = "s"
+HS_ENG = "v"
+LAST_A = 0
+
+
+def is_c(n):
+    return C_EVERY > 0 and n % C_EVERY == C_PHASE and n < NPAIR - LAST_A
+
+
+def tile_lstmcell_t_kernel(tc, x, h, c, Wx, Wh, bx, bh, out_0, out_1):
+    nc = tc.nc
+    x_v = x.rearrange("(p t) k -> p (t k)", t=NT)
+    h_v = h.rearrange("(p t) k -> p (t k)", t=NT)
+    c_v = c.rearrange("(p t) k -> p (t k)", t=NT)
+    hs_v = out_0.rearrange("(p t) k -> p (t k)", t=NT)
+    cn_v = out_1.rearrange("(p t) k -> p (t k)", t=NT)
+
+    with ExitStack() as ctx:
+        const = ctx.enter_context(tc.tile_pool(name="const", bufs=1))
+        work = ctx.enter_context(tc.tile_pool(name="work", bufs=1))
+        psum = ctx.enter_context(tc.psum_pool(name="psum", bufs=1))
+        if PIN:
+            ctx.enter_context(tc.manual_schedule())
+
+        eng = {"v": nc.vector, "g": nc.gpsimd}
+
+        wh_sb = const.tile([P, G4], BF16, name="wh_sb")
+        nc.scalar.dma_start(out=wh_sb[:].rearrange("n (a k) -> n a k", a=4), in_=Wh.rearrange("a n k -> n a k"))
+        brows = []
+        for b_in in (bx, bh):
+            t = const.tile([P, P], BF16, name="brow%d" % len(brows))
+            nc.vector.memset(t[:], 0.0)
+            nc.scalar.dma_start(out=t[0:4, :], in_=b_in)
+            brows.append(t)
+
+        w_sb = const.tile([P, 4 * I], BF16, name="w_sb")
+        xs = {}
+        h_sb = {}
+        c_sb = {}
+
+        def load_w(hf):
+            nc.sync.dma_start(out=w_sb[:, hf * 2 * I:(hf + 1) * 2 * I].rearrange("n (a k) -> n a k", a=2),
+                              in_=Wx[2 * hf:2 * hf + 2].rearrange("a n k -> n a k"))
+
+        def load_x(q, lo, hi):
+            if q not in xs:
+                xs[q] = work.tile([P, 4 * I], BF16, tag="xs", bufs=4, name="xs")
+            nc.sync.dma_start(out=xs[q][:, lo * I:hi * I], in_=x_v[:, (4 * q + lo) * I:(4 * q + hi) * I])
+
+        def load_hc(ch, which):
+            if which == "h":
+                t = const.tile([P, 16 * H], BF16, name="h_sb%d" % ch)
+                nc.sync.dma_start(out=t[:], in_=h_v[:, ch * 16 * H:(ch + 1) * 16 * H])
+                h_sb[ch] = t
+            else:
+                t = const.tile([P, 16 * H], BF16, name="c_sb%d" % ch)
+                nc.sync.dma_start(out=t[:], in_=c_v[:, ch * 16 * H:(ch + 1) * 16 * H])
+                c_sb[ch] = t
+
+        load_w(0)
+        load_w(1)
+        load_x(0, 0, 2)
+        load_hc(0, "h")
+        load_x(0, 2, 4)
+        load_x(1, 0, 4)
+        load_x(2, 0, 4)
+        load_hc(0, "c")
+
+        warm = const.tile([P, 1], F32, name="warm")
+        nc.vector.memset(warm[:], 0.0)
+        nc.scalar.activation(out=warm[:], in_=warm[:], func=AF.Sigmoid)
+
+        ident_f = const.tile([P, P], F32, name="ident_f")
+        make_identity(nc, ident_f[:])
+        ident_b = const.tile([P, P], BF16, name="ident_b")
+        make_identity(nc, ident_b[:])
+
+        xts = {}
+        grps = {}
+        codes = {}
+        scls = {}
+        hTs = {}
+        ghs = {}
+        gxs = {}
+        gxsb = {}
+        gqs = {}
+        t1s = {}
+        t2s = {}
+        cns = {}
+        ths = {}
+
+        w32 = w_sb[:].bitcast(F32)
+        wgrp = const.tile([P, 2 * G4 * 4], BF16, name="wgrp", align_bytes=64)
+        wgrp32 = wgrp[:].bitcast(F32).rearrange("p (g n u) -> p g n u", g=2, u=2)
+        wc = const.tile([P, 2 * G4], U32, name="wc", align_bytes=64)
+        ws = const.tile([P, 2 * G4], U8, name="ws", align_bytes=64)
+        whT = const.tile([P, G4], BF16, name="whT")
+        biasT = const.tile([P, 4], F32, name="biasT")
+        bias_bc = const.tile([P, G4], F32, name="bias_bc")
+
+        def prep_w(a, who):
+            wt = psum.tile([P, 4, P], F32, tag="xt", bufs=XT_BUFS, name="wt")
+            for gu in range(4):
+                nc.tensor.transpose(wt[:, gu, :], w32[:, a * 512 + (gu // 2) * 256 + gu % 2:a * 512 + (gu // 2 + 1) * 256:2], ident_f[:])
+            dst = wgrp32[:, :, POS[a] * P:(POS[a] + 1) * P, :]
+            src = wt[:].rearrange("p (g u) n -> p g n u", g=2)
+            if who == "s":
+                nc.scalar.copy(out=dst, in_=src)
+            else:
+                nc.vector.tensor_copy(out=dst, in_=src)
+
+        def quant_w():
+            for g in range(2):
+                nc.vector.quantize_mx(out=wc[:, g * G4:(g + 1) * G4].bitcast(FP8X4), scales=ws[:, g * G4:(g + 1) * G4],
+                                      in_=wgrp[:, g * 4 * G4:(g + 1) * 4 * G4])
+
+        def prep_small():
+            wht_ps = psum.tile([P, 8, P], BF16, tag="xt", bufs=XT_BUFS, name="wht_ps")
+            for a in range(4):
+                nc.tensor.transpose(wht_ps[:, POS[a], :], wh_sb[:, a * P:(a + 1) * P], ident_b[:])
+            for i in range(2):
+                nc.tensor.transpose(wht_ps[:, 4 + i, :], brows[i][:], ident_b[:])
+            nc.vector.tensor_copy(out=whT[:], in_=wht_ps[:, 0:4, :].rearrange("k a n -> k (a n)"))
+            bc_sb = const.tile([P, 2, 4], F32, name="bc_sb")
+            nc.vector.tensor_copy(out=bc_sb[:], in_=wht_ps[:, 4:6, 0:4])
+            nc.vector.tensor_tensor(out=biasT[:], in0=bc_sb[:, 0, :], in1=bc_sb[:, 1, :], op=ALU.add)
+            b_ps = psum.tile([P, G4], F32, tag="ghc", bufs=2, name="b_ps")
+            for a in range(4):
+                for i in range(2):
+                    nc.tensor.matmul(b_ps[:, POS[a] * P:(POS[a] + 1) * P], lhsT=ident_b[:, a:a + 1].to_broadcast([P, P]),
+                                     rhs=brows[i][:], start=(i == 0), stop=(i == 1))
+            nc.vector.tensor_copy(out=bias_bc[:], in_=b_ps[:])
+
+        def st_T(n):
+            q, half = divmod(n, 2)
+            x32 = xs[q][:].bitcast(F32)
+            for jj in range(2):
+                j4 = 2 * half + jj
+                xt = psum.tile([P, 4, P], F32, tag="xt", bufs=XT_BUFS, name="xt")
+                for gu in range(4):
+                    nc.tensor.transpose(xt[:, gu, :], x32[:, j4 * 512 + (gu // 2) * 256 + gu % 2:j4 * 512 + (gu // 2 + 1) * 256:2], ident_f[:])
+                xts[(n, jj)] = xt
+
+        def st_XC(n, who):
+            q, half = divmod(n, 2)
+            if q not in grps:
+                grps[q] = work.tile([P, 4096], BF16, tag="grp", bufs=GRP_BUFS, name="grp", align_bytes=64)
+            g32 = grps[q][:].bitcast(F32).rearrange("p (f g j b u) -> p f g j b u", f=2, g=2, j=2, u=2)
+            for jj in range(2):
+                src = xts[(n, jj)][:].rearrange("p (g u) b -> p g b u", g=2)
+                if who[jj] == "s":
+                    nc.scalar.copy(out=g32[:, half, :, jj, :, :], in_=src)
+                else:
+                    nc.vector.tensor_copy(out=g32[:, half, :, jj, :, :], in_=src)
+
+        def st_Q(q, lo, hi):
+            if q not in codes:
+                codes[q] = work.tile([P, 1024], U32, tag="codes", bufs=3, name="cd", align_bytes=64)
+                scls[q] = work.tile([P, 1024], U8, tag="scl", bufs=3, name="sc", align_bytes=64)
+            nc.vector.quantize_mx(out=codes[q][:, lo * 512:hi * 512].bitcast(FP8X4), scales=scls[q][:, lo * 512:hi * 512],
+                                  in_=grps[q][:, lo * 2048:hi * 2048])
+
+        def st_HT(o, who):
+            hps = psum.tile([P, 8, P], BF16, tag="xt", bufs=XT_BUFS, name="hps")
+            for k8 in range(8):
+                ch, jc = divmod(8 * o + k8, 16)
+                nc.tensor.transpose(hps[:, k8, :], h_sb[ch][:, jc * P:(jc + 1) * P], ident_b[:])
+            hT = work.tile([P, 8 * P], BF16, tag="hT", bufs=3, name="hT")
+            if who == "s":
+                nc.scalar.copy(out=hT[:], in_=hps[:].rearrange("k j b -> k (j b)"))
+            else:
+                nc.vector.tensor_copy(out=hT[:], in_=hps[:].rearrange("k j b -> k (j b)"))
+            hTs[o] = hT
+
+        def gq_of(n):
+            q = n // 2
+            if q not in gqs:
+                gqs[q] = work.tile([P, 4 * G4], F32, tag="gq", bufs=GQ_BUFS, name="gq")
+            return gqs[q]
+
+        def st_GHmm(n, jj):
+            o, k8 = divmod(2 * n + jj, 8)
+            if is_c(n):
+                gh = psum.tile([P, G4], F32, tag="ghc", bufs=2, name="ghc")
+            else:
+                gh = psum.tile([P, G4], F32, tag=("xt" if GHA_BUFS == 0 else "gha"), bufs=(XT_BUFS if GHA_BUFS == 0 else GHA_BUFS), name="gha")
+            nc.tensor.matmul(gh[:], lhsT=hTs[o][:, k8 * P:(k8 + 1) * P], rhs=whT[:], start=True, stop=not is_c(n))
+            ghs[(n, jj)] = gh
+
+        def st_GHadd(n, jj):
+            for pos in range(4):
+                nc.tensor.matmul(ghs[(n, jj)][:, pos * P:(pos + 1) * P],
+                                 lhsT=gxsb[n][:, pos * 256 + jj * P:pos * 256 + (jj + 1) * P],
+                                 rhs=ident_f[:], is_transpose=True, start=False, stop=(pos == 3))
+
+        def st_GB(n, jj):
+            gq = gq_of(n)
+            j4 = 2 * (n % 2) + jj
+            nc.vector.tensor_tensor(out=gq[:, j4 * G4:(j4 + 1) * G4], in0=ghs[(n, jj)][:], in1=bias_bc[:], op=ALU.add)
+
+        def st_MX(n):
+            q, half = divmod(n, 2)
+            cd, sc = codes[q], scls[q]
+            o0 = half * 512
+            if is_c(n):
+                for bk in range(2):
+                    gx = psum.tile([P, G4], F32, tag="gx", bufs=GX_BUFS, name="gx")
+                    for hf in range(2):
+                        pos = 2 * bk + hf
+                        for g in range(2):
+                            wsl = slice(g * G4 + pos * P, g * G4 + (pos + 1) * P)
+                            xsl = slice(o0 + g * 256, o0 + (g + 1) * 256)
+                            nc.tensor.matmul_mx(out=gx[:, hf * 256:(hf + 1) * 256],
+                                                lhsT=wc[:, wsl].bitcast(FP8X4), lhsT_scale=ws[:, wsl],
+                                                rhs=cd[:, xsl].bitcast(FP8X4), rhs_scale=sc[:, xsl],
+                                                start=(g == 0), stop=(g == 1))
+                    gxs[(n, bk)] = gx
+            else:
+                for jj in range(2):
+                    gx = psum.tile([P, G4], F32, tag="gx", bufs=GX_BUFS, name="gx")
+                    for g in range(2):
+                        xsl = slice(o0 + (2 * g + jj) * P, o0 + (2 * g + jj + 1) * P)
+                        wsl = slice(g * G4, (g + 1) * G4)
+                        nc.tensor.matmul_mx(out=gx[:], lhsT=cd[:, xsl].bitcast(FP8X4), lhsT_scale=sc[:, xsl],
+                                            rhs=wc[:, wsl].bitcast(FP8X4), rhs_scale=ws[:, wsl],
+                                            start=(g == 0), stop=(g == 1))
+                    gxs[(n, jj)] = gx
+
+        def st_AD(n, jj):
+            gq = gq_of(n)
+            j4 = 2 * (n % 2) + jj
+            sl = gq[:, j4 * G4:(j4 + 1) * G4]
+            nc.vector.tensor_tensor(out=sl, in0=gxs[(n, jj)][:], in1=sl, op=ALU.add)
+
+        def st_CP(n, bk, who):
+            if n not in gxsb:
+                gxsb[n] = work.tile([P, 4 * 256], F32, tag="gxsb", bufs=2, name="gxsb")
+            t = gxsb[n]
+            for hf in range(2):
+                pos = 2 * bk + hf
+                a = INV[pos]
+                if who == "v":
+                    nc.vector.tensor_scalar_add(out=t[:, pos * 256:(pos + 1) * 256],
+                                                in0=gxs[(n, bk)][:, hf * 256:(hf + 1) * 256], scalar1=biasT[:, a:a + 1])
+                else:
+                    nc.scalar.activation(out=t[:, pos * 256:(pos + 1) * 256],
+                                         in_=gxs[(n, bk)][:, hf * 256:(hf + 1) * 256], func=AF.Identity,
+                                         bias=biasT[:, a:a + 1])
+
+        def st_ACT(n):
+            gq = gq_of(n)
+            if is_c(n):
+                for jj in range(2):
+                    j4 = 2 * (n % 2) + jj
+                    nc.scalar.activation(out=gq[:, j4 * G4:j4 * G4 + 384], in_=ghs[(n, jj)][:, 0:384], func=AF.Sigmoid)
+                    nc.scalar.activation(out=gq[:, j4 * G4 + 384:(j4 + 1) * G4], in_=ghs[(n, jj)][:, 384:512], func=AF.Tanh)
+            else:
+                g3 = gq[:].rearrange("p (j n) -> p j n", j=4)
+                j0 = 2 * (n % 2)
+                nc.scalar.activation(out=g3[:, j0:j0 + 2, 0:384], in_=g3[:, j0:j0 + 2, 0:384], func=AF.Sigmoid)
+                nc.scalar.activation(out=g3[:, j0:j0 + 2, 384:512], in_=g3[:, j0:j0 + 2, 384:512], func=AF.Tanh)
+
+        def gview(u):
+            q, j0, nj = u
+            return gqs[q][:].rearrange("p (j n) -> p j n", j=4)[:, j0:j0 + nj, :]
+
+        def v3(t, u):
+            return t[:, 0:u[2] * H].rearrange("p (j n) -> p j n", j=u[2])
+
+        def st_t1(u, e):
+            q, j0, nj = u
+            ch, q4 = divmod(q, 4)
+            c3 = c_sb[ch][:, q4 * 512 + j0 * H:q4 * 512 + (j0 + nj) * H].rearrange("p (j n) -> p j n", j=nj)
+            t1s[u] = work.tile([P, nj * H], F32, tag="t1_%d" % nj, bufs=(T1_BUFS if nj == 4 else 2), name="t1")
+            eng[e].tensor_tensor(out=v3(t1s[u], u), in0=gview(u)[:, :, 128:256], in1=c3, op=ALU.mult)
+
+        def st_t2(u, e):
+            t2s[u] = work.tile([P, u[2] * H], F32, tag="t2_%d" % u[2], bufs=(T2_BUFS if u[2] == 4 else 2), name="t2")
+            eng[e].tensor_tensor(out=v3(t2s[u], u), in0=gview(u)[:, :, 0:128], in1=gview(u)[:, :, 384:512], op=ALU.mult)
+
+        def st_cn(u, e):
+            q, j0, nj = u
+            w = nj * H
+            cn = work.tile([P, 512], F32, tag="cn", bufs=5, name="cn")
+            eng[e].tensor_tensor(out=cn[:, 0:w], in0=t1s[u][:, 0:w], in1=t2s[u][:, 0:w], op=ALU.add)
+            nc.sync.dma_start(out=cn_v[:, q * 512 + j0 * H:q * 512 + (j0 + nj) * H], in_=cn[:, 0:w])
+            cns[u] = cn
+
+        def st_TC(u):
+            w = u[2] * H
+            th = work.tile([P, 512], F32, tag="th", bufs=2, name="th")
+            nc.scalar.activation(out=th[:, 0:w], in_=cns[u][:, 0:w], func=AF.Tanh)
+            ths[u] = th
+
+        def st_hs(u, e):
+            q, j0, nj = u
+            w = nj * H
+            hs = work.tile([P, 512], F32, tag="hs", bufs=5, name="hs")
+            eng[e].tensor_tensor(out=v3(hs, u), in0=gview(u)[:, :, 256:384], in1=v3(ths[u], u), op=ALU.mult)
+            nc.sync.dma_start(out=hs_v[:, q * 512 + j0 * H:q * 512 + (j0 + nj) * H], in_=hs[:, 0:w])
+
+        prep_small()
+        prep_w(0, "s")
+        prep_w(1, "v")
+        prep_w(2, "s")
+        prep_w(3, "v")
+        st_T(0)
+        st_XC(0, "ss")
+        quant_w()
+        st_Q(0, 0, 1)
+        st_HT(0, "s")
+        st_T(1)
+        st_XC(1, "sv")
+
+        def quad(q):
+            return (q, 0, 4)
+
+        def pair(n):
+            return (n // 2, 2 * (n % 2), 2)
+
+        def tmax(m):
+            return min(m + LOOK, 2 * m + 1, NPAIR - 1)
+
+        NSTEADY = NQUAD - 2
+
+        def hs_eng(q):
+            if q >= NSTEADY - 1 or HS_ENG == "v":
+                return "v"
+            if HS_ENG == "g":
+                return "g"
+            return "g" if q % 2 == int(HS_ENG) else "v"
+
+        for m in range(NPAIR):
+            p2 = m - 2
+            if p2 >= 0 and is_c(p2):
+                st_GHadd(p2, 0)
+                st_GHadd(p2, 1)
+                st_ACT(p2)
+            if m > 0:
+                for n in range(tmax(m - 1) + 1, tmax(m) + 1):
+                    if n % 2 == 0 and 3 <= n // 2 + 2 < NQUAD:
+                        load_x(n // 2 + 2, 0, 4)
+                    if n % 8 == 2 and n // 8 + 1 < 4:
+                        load_hc(n // 8 + 1, "h")
+                        load_hc(n // 8 + 1, "c")
+                    st_T(n)
+                    st_XC(n, (XCE if n % 2 == 0 else XCO) if n >= 6 else "sv")
+                    if (n + 2) % 4 == 0 and (n + 2) // 4 < 8:
+                        st_HT((n + 2) // 4, HTE)
+            if p2 >= 0 and not is_c(p2):
+                st_ACT(p2)
+            st_GHmm(m, 0)
+            if not is_c(m):
+                st_GB(m, 0)
+            if m == 0:
+                st_Q(0, 1, 2)
+            if m % 2 == 1:
+                if (m + 1) // 2 < NQUAD:
+                    st_Q((m + 1) // 2, 0, 2)
+                q = (m - 5) // 2
+                if 0 <= q - 1 < NSTEADY and hs_eng(q - 1) == "v":
+                    st_hs(quad(q - 1), "v")
+                if 0 <= q < NSTEADY:
+                    st_cn(quad(q), "v")
+                if 0 <= q + 1 < NSTEADY:
+                    st_t1(quad(q + 1), "g")
+                    st_t2(quad(q + 1), "g")
+                if 0 <= q < NSTEADY and hs_eng(q) == "g":
+                    st_TC(quad(q))
+                    st_hs(quad(q), "g")
+            st_MX(m)
+            st_GHmm(m, 1)
+            if is_c(m):
+                st_CP(m, 0, CP0 if (m // 2) % 2 == 0 else CP0B)
+                st_CP(m, 1, "s" if m >= NPAIR - TAIL_S else (CP1 if (m // 2) % 2 == 0 else CP1B))
+            else:
+                st_AD(m, 0)
+                st_GB(m, 1)
+                st_AD(m, 1)
+            if m % 2 == 1 and 0 <= (m - 5) // 2 < NSTEADY and hs_eng((m - 5) // 2) == "v":
+                st_TC(quad((m - 5) // 2))
+
+        last = NPAIR - 1
+        st_GHadd(last, 0)
+        st_GHadd(last, 1)
+        st_ACT(last - 1)
+        st_ACT(last)
+        units = [quad(NQUAD - 3), quad(NQUAD - 2), pair(last - 1), pair(last)]
+        for i in range(1, len(units) + 1):
+            if i < len(units):
+                st_t1(units[i], "v")
+                st_t2(units[i], "v")
+                st_cn(units[i], "v")
+                st_TC(units[i])
+            st_hs(units[i - 1], "v")

@@ -24,7 +24,6 @@ INV = (0, 1, 3, 2)
 PIN = True
 XT_BUFS = 4
 GX_BUFS = 2
-GHA_BUFS = 0
 LOOK = 3
 OFF = 3
 NTAILQ = 2
@@ -95,11 +94,11 @@ def tile_lstmcell_t_kernel(tc, x, h, c, Wx, Wh, bx, bh, out_0, out_1):
                 xs[q] = work.tile([P, 4 * I], BF16, tag="xs", bufs=4, name="xs")
             nc.sync.dma_start(out=xs[q][:, lo * I:hi * I], in_=x_v[:, (4 * q + lo) * I:(4 * q + hi) * I])
 
-        def load_hc(ch, which):
+        def load_hc(ch, which, lo=0, hi=16):
             if which == "h":
-                t = const.tile([P, 16 * H], BF16, name="h_sb%d" % ch)
-                nc.sync.dma_start(out=t[:], in_=h_v[:, ch * 16 * H:(ch + 1) * 16 * H])
-                h_sb[ch] = t
+                if ch not in h_sb:
+                    h_sb[ch] = const.tile([P, 16 * H], BF16, name="h_sb%d" % ch)
+                nc.sync.dma_start(out=h_sb[ch][:, lo * H:hi * H], in_=h_v[:, (ch * 16 + lo) * H:(ch * 16 + hi) * H])
             else:
                 t = const.tile([P, 16 * H], BF16, name="c_sb%d" % ch)
                 nc.sync.dma_start(out=t[:], in_=c_v[:, ch * 16 * H:(ch + 1) * 16 * H])
@@ -108,9 +107,10 @@ def tile_lstmcell_t_kernel(tc, x, h, c, Wx, Wh, bx, bh, out_0, out_1):
         load_w(0)
         load_w(1)
         load_x(0, 0, 2)
-        load_hc(0, "h")
+        load_hc(0, "h", 0, 8)
         load_x(0, 2, 4)
         load_x(1, 0, 4)
+        load_hc(0, "h", 8, 16)
         load_x(2, 0, 4)
         load_hc(0, "c")
 
@@ -162,15 +162,18 @@ def tile_lstmcell_t_kernel(tc, x, h, c, Wx, Wh, bx, bh, out_0, out_1):
                 nc.vector.quantize_mx(out=wc[:, g * G4:(g + 1) * G4].bitcast(FP8X4), scales=ws[:, g * G4:(g + 1) * G4],
                                       in_=wgrp[:, g * 4 * G4:(g + 1) * 4 * G4])
 
-        def prep_small():
-            wht_ps = psum.tile([P, 8, P], BF16, tag="xt", bufs=XT_BUFS, name="wht_ps")
+        def prep_wh():
+            wht_ps = psum.tile([P, 4, P], BF16, tag="gx", bufs=GX_BUFS, name="wht_ps")
             for a in range(4):
                 nc.tensor.transpose(wht_ps[:, POS[a], :], wh_sb[:, a * P:(a + 1) * P], ident_b[:])
+            nc.vector.tensor_copy(out=whT[:], in_=wht_ps[:].rearrange("k a n -> k (a n)"))
+
+        def prep_bias():
+            bc_ps = psum.tile([P, 2, P], BF16, tag="ghc", bufs=2, name="bc_ps")
             for i in range(2):
-                nc.tensor.transpose(wht_ps[:, 4 + i, :], brows[i][:], ident_b[:])
-            nc.vector.tensor_copy(out=whT[:], in_=wht_ps[:, 0:4, :].rearrange("k a n -> k (a n)"))
+                nc.tensor.transpose(bc_ps[:, i, :], brows[i][:], ident_b[:])
             bc_sb = const.tile([P, 2, 4], F32, name="bc_sb")
-            nc.vector.tensor_copy(out=bc_sb[:], in_=wht_ps[:, 4:6, 0:4])
+            nc.vector.tensor_copy(out=bc_sb[:], in_=bc_ps[:, :, 0:4])
             nc.vector.tensor_tensor(out=biasT[:], in0=bc_sb[:, 0, :], in1=bc_sb[:, 1, :], op=ALU.add)
             b_ps = psum.tile([P, G4], F32, tag="ghc", bufs=2, name="b_ps")
             for a in range(4):
@@ -231,7 +234,7 @@ def tile_lstmcell_t_kernel(tc, x, h, c, Wx, Wh, bx, bh, out_0, out_1):
             if is_c(n):
                 gh = psum.tile([P, G4], F32, tag="ghc", bufs=2, name="ghc")
             else:
-                gh = psum.tile([P, G4], F32, tag=("xt" if GHA_BUFS == 0 else "gha"), bufs=(XT_BUFS if GHA_BUFS == 0 else GHA_BUFS), name="gha")
+                gh = psum.tile([P, G4], F32, tag="xt", bufs=XT_BUFS, name="gha")
             nc.tensor.matmul(gh[:], lhsT=hTs[o][:, k8 * P:(k8 + 1) * P], rhs=whT[:], start=True, stop=not is_c(n))
             ghs[(n, jj)] = gh
 
@@ -347,7 +350,7 @@ def tile_lstmcell_t_kernel(tc, x, h, c, Wx, Wh, bx, bh, out_0, out_1):
             eng[e].tensor_tensor(out=v3(hs, u), in0=gview(u)[:, :, 256:384], in1=v3(ths[u], u), op=ALU.mult)
             nc.sync.dma_start(out=hs_v[:, q * 512 + j0 * H:q * 512 + (j0 + nj) * H], in_=hs[:, 0:w])
 
-        prep_small()
+        prep_wh()
         prep_w(0, "s")
         prep_w(1, "v")
         prep_w(2, "s")
@@ -357,6 +360,7 @@ def tile_lstmcell_t_kernel(tc, x, h, c, Wx, Wh, bx, bh, out_0, out_1):
         quant_w()
         st_Q(0, 0, 1)
         st_HT(0, "s")
+        prep_bias()
         st_T(1)
         st_XC(1, "sv")
 

@@ -48,10 +48,14 @@ CP1B = "s"
 HTE = "s"
 HS_ENG = "v"
 LAST_A = 0
+NOT_C = ()
+ALSO_C = (30,)
+XT_C = (30, 31)
+XS_BUFS = 4
 
 
 def is_c(n):
-    return C_EVERY > 0 and n % C_EVERY == C_PHASE and n < NPAIR - LAST_A
+    return (n % C_EVERY == C_PHASE and n not in NOT_C) or n in ALSO_C
 
 
 def tile_lstmcell_t_kernel(tc, x, h, c, Wx, Wh, bx, bh, out_0, out_1):
@@ -73,25 +77,21 @@ def tile_lstmcell_t_kernel(tc, x, h, c, Wx, Wh, bx, bh, out_0, out_1):
 
         wh_sb = const.tile([P, G4], BF16, name="wh_sb")
         nc.scalar.dma_start(out=wh_sb[:].rearrange("n (a k) -> n a k", a=4), in_=Wh.rearrange("a n k -> n a k"))
-        brows = []
-        for b_in in (bx, bh):
-            t = const.tile([P, P], BF16, name="brow%d" % len(brows))
-            nc.vector.memset(t[:], 0.0)
-            nc.scalar.dma_start(out=t[0:4, :], in_=b_in)
-            brows.append(t)
+        brow = const.tile([P, G4], BF16, name="brow")
+        nc.vector.memset(brow[:], 0.0)
+        for i, b_in in enumerate((bx, bh)):
+            nc.scalar.dma_start(out=brow[i:i + 1, :], in_=b_in.rearrange("(i a) n -> i (a n)", i=1))
+        ones = const.tile([P, P], BF16, name="ones")
+        nc.vector.memset(ones[:], 1.0)
 
         w_sb = const.tile([P, 4 * I], BF16, name="w_sb")
         xs = {}
         h_sb = {}
         c_sb = {}
 
-        def load_w(hf):
-            nc.sync.dma_start(out=w_sb[:, hf * 2 * I:(hf + 1) * 2 * I].rearrange("n (a k) -> n a k", a=2),
-                              in_=Wx[2 * hf:2 * hf + 2].rearrange("a n k -> n a k"))
-
         def load_x(q, lo, hi):
             if q not in xs:
-                xs[q] = work.tile([P, 4 * I], BF16, tag="xs", bufs=4, name="xs")
+                xs[q] = work.tile([P, 4 * I], BF16, tag="xs", bufs=XS_BUFS, name="xs")
             nc.sync.dma_start(out=xs[q][:, lo * I:hi * I], in_=x_v[:, (4 * q + lo) * I:(4 * q + hi) * I])
 
         def load_hc(ch, which, lo=0, hi=16):
@@ -104,8 +104,8 @@ def tile_lstmcell_t_kernel(tc, x, h, c, Wx, Wh, bx, bh, out_0, out_1):
                 nc.sync.dma_start(out=t[:], in_=c_v[:, ch * 16 * H:(ch + 1) * 16 * H])
                 c_sb[ch] = t
 
-        load_w(0)
-        load_w(1)
+        for a in range(4):
+            nc.sync.dma_start(out=w_sb[:, a * I:(a + 1) * I], in_=Wx[a])
         load_x(0, 0, 2)
         load_hc(0, "h", 0, 8)
         load_x(0, 2, 4)
@@ -169,18 +169,17 @@ def tile_lstmcell_t_kernel(tc, x, h, c, Wx, Wh, bx, bh, out_0, out_1):
             nc.vector.tensor_copy(out=whT[:], in_=wht_ps[:].rearrange("k a n -> k (a n)"))
 
         def prep_bias():
-            bc_ps = psum.tile([P, 2, P], BF16, tag="ghc", bufs=2, name="bc_ps")
-            for i in range(2):
-                nc.tensor.transpose(bc_ps[:, i, :], brows[i][:], ident_b[:])
-            bc_sb = const.tile([P, 2, 4], F32, name="bc_sb")
-            nc.vector.tensor_copy(out=bc_sb[:], in_=bc_ps[:, :, 0:4])
-            nc.vector.tensor_tensor(out=biasT[:], in0=bc_sb[:, 0, :], in1=bc_sb[:, 1, :], op=ALU.add)
-            b_ps = psum.tile([P, G4], F32, tag="ghc", bufs=2, name="b_ps")
+            bc_ps = psum.tile([P, 4, P], BF16, tag="ghc", bufs=2, name="bc_ps")
             for a in range(4):
-                for i in range(2):
-                    nc.tensor.matmul(b_ps[:, POS[a] * P:(POS[a] + 1) * P], lhsT=ident_b[:, a:a + 1].to_broadcast([P, P]),
-                                     rhs=brows[i][:], start=(i == 0), stop=(i == 1))
-            nc.vector.tensor_copy(out=bias_bc[:], in_=b_ps[:])
+                nc.tensor.transpose(bc_ps[:, a, :], brow[:, a * P:(a + 1) * P], ident_b[:])
+            bc_sb = const.tile([P, 4, 2], F32, name="bc_sb")
+            nc.vector.tensor_copy(out=bc_sb[:], in_=bc_ps[:, :, 0:2])
+            b_ps = psum.tile([P, G4], F32, tag="ghc", bufs=2, name="b_ps")
+            nc.tensor.matmul(b_ps[:], lhsT=ones[:], rhs=brow[:], start=True, stop=True)
+            nc.vector.tensor_tensor(out=biasT[:], in0=bc_sb[:, :, 0], in1=bc_sb[:, :, 1], op=ALU.add)
+            nc.vector.tensor_copy(out=bias_bc[:, 0:256], in_=b_ps[:, 0:256])
+            nc.vector.tensor_copy(out=bias_bc[:, 256:384], in_=b_ps[:, 384:512])
+            nc.vector.tensor_copy(out=bias_bc[:, 384:512], in_=b_ps[:, 256:384])
 
         def st_T(n):
             q, half = divmod(n, 2)
@@ -231,7 +230,7 @@ def tile_lstmcell_t_kernel(tc, x, h, c, Wx, Wh, bx, bh, out_0, out_1):
 
         def st_GHmm(n, jj):
             o, k8 = divmod(2 * n + jj, 8)
-            if is_c(n):
+            if is_c(n) and n not in XT_C:
                 gh = psum.tile([P, G4], F32, tag="ghc", bufs=2, name="ghc")
             else:
                 gh = psum.tile([P, G4], F32, tag="xt", bufs=XT_BUFS, name="gha")
@@ -298,10 +297,10 @@ def tile_lstmcell_t_kernel(tc, x, h, c, Wx, Wh, bx, bh, out_0, out_1):
                                          in_=gxs[(n, bk)][:, hf * 256:(hf + 1) * 256], func=AF.Identity,
                                          bias=biasT[:, a:a + 1])
 
-        def st_ACT(n):
+        def st_ACT(n, tiles=(0, 1)):
             gq = gq_of(n)
             if is_c(n):
-                for jj in range(2):
+                for jj in tiles:
                     j4 = 2 * (n % 2) + jj
                     nc.scalar.activation(out=gq[:, j4 * G4:j4 * G4 + 384], in_=ghs[(n, jj)][:, 0:384], func=AF.Sigmoid)
                     nc.scalar.activation(out=gq[:, j4 * G4 + 384:(j4 + 1) * G4], in_=ghs[(n, jj)][:, 384:512], func=AF.Tanh)
@@ -415,8 +414,8 @@ def tile_lstmcell_t_kernel(tc, x, h, c, Wx, Wh, bx, bh, out_0, out_1):
                 if 0 <= q < NSTEADY:
                     st_cn(quad(q), "v")
                 if 0 <= q + 1 < NSTEADY:
-                    st_t1(quad(q + 1), "g")
-                    st_t2(quad(q + 1), "g")
+                    st_t1(quad(q + 1), "g" if q + 1 < NSTEADY - 1 else "v")
+                    st_t2(quad(q + 1), "g" if q + 1 < NSTEADY - 1 else "v")
                 if 0 <= q < NSTEADY and hs_eng(q) == "g":
                     st_TC(quad(q))
                     st_hs(quad(q), "g")
@@ -433,15 +432,34 @@ def tile_lstmcell_t_kernel(tc, x, h, c, Wx, Wh, bx, bh, out_0, out_1):
                 st_TC(quad((m - 5) // 2))
 
         last = NPAIR - 1
-        st_GHadd(last, 0)
-        st_GHadd(last, 1)
-        st_ACT(last - 1)
-        st_ACT(last)
-        units = [quad(NQUAD - 3), quad(NQUAD - 2), pair(last - 1), pair(last)]
-        for i in range(1, len(units) + 1):
-            if i < len(units):
-                st_t1(units[i], "v")
-                st_t2(units[i], "v")
-                st_cn(units[i], "v")
-                st_TC(units[i])
-            st_hs(units[i - 1], "v")
+        q14 = quad(NQUAD - 2)
+        ta, tb = (NQUAD - 1, 2, 1), (NQUAD - 1, 3, 1)
+        p30 = pair(last - 1)
+        st_GHadd(30, 0)
+        st_GHadd(30, 1)
+        st_ACT(30)
+        st_t1(q14, "v")
+        st_t2(q14, "v")
+        st_hs(quad(NQUAD - 3), "v")
+        st_cn(q14, "v")
+        st_GHadd(31, 0)
+        st_GHadd(31, 1)
+        st_ACT(31, (0,))
+        st_TC(q14)
+        st_t1(p30, "v")
+        st_t2(p30, "v")
+        st_ACT(31, (1,))
+        st_cn(p30, "v")
+        st_t1(ta, "v")
+        st_TC(p30)
+        st_t2(ta, "v")
+        st_hs(q14, "v")
+        st_cn(ta, "v")
+        st_t1(tb, "v")
+        st_TC(ta)
+        st_t2(tb, "v")
+        st_hs(p30, "v")
+        st_cn(tb, "v")
+        st_TC(tb)
+        st_hs(ta, "v")
+        st_hs(tb, "v")

from contextlib import ExitStack

import concourse.mybir as mybir
from concourse.masks import make_identity

F32 = mybir.dt.float32
BF16 = mybir.dt.bfloat16
U32 = mybir.dt.uint32
U8 = mybir.dt.uint8
FP8X4 = mybir.dt.float8_e4m3fn_x4
AF = mybir.ActivationFunctionType
ALU = mybir.AluOpType

P = 128
B, I, H = 8192, 1024, 128
NT = B // P
NPAIR = NT // 2
NQUAD = NT // 4
G4 = 4 * H
FLOPS = 2 * B * (I + H) * G4
POS = (0, 1, 3, 2)
INV = (0, 1, 3, 2)

PIN = True
XT_BUFS = 4
GX_BUFS = 2
LOOK = 3
OFF = 3
NTAILQ = 2
C_EVERY = 2
C_PHASE = 1
GRP_BUFS = 3
GQ_BUFS = 6
T2_BUFS = 1
T1_BUFS = 1
CP1 = "s"
TAIL_S = 1


HEAD_RAMP = 1
QWHOLE = 2
LASTW = NQUAD - 3
XCE = "ss"
XCO = "sv"
CP0 = "s"
CP0B = "v"
CP1B = "s"
HTE = "s"
HS_ENG = "v"
LAST_A = 0
NOT_C = ()
ALSO_C = (30,)
XT_C = (30, 31)
XS_BUFS = 4


def is_c(n):
    return (n % C_EVERY == C_PHASE and n not in NOT_C) or n in ALSO_C


def tile_lstmcell_t_kernel(tc, x, h, c, Wx, Wh, bx, bh, out_0, out_1):
    nc = tc.nc
    x_v = x.rearrange("(p t) k -> p (t k)", t=NT)
    h_v = h.rearrange("(p t) k -> p (t k)", t=NT)
    c_v = c.rearrange("(p t) k -> p (t k)", t=NT)
    hs_v = out_0.rearrange("(p t) k -> p (t k)", t=NT)
    cn_v = out_1.rearrange("(p t) k -> p (t k)", t=NT)

    with ExitStack() as ctx:
        const = ctx.enter_context(tc.tile_pool(name="const", bufs=1))
        work = ctx.enter_context(tc.tile_pool(name="work", bufs=1))
        psum = ctx.enter_context(tc.psum_pool(name="psum", bufs=1))
        if PIN:
            ctx.enter_context(tc.manual_schedule())

        eng = {"v": nc.vector, "g": nc.gpsimd}

        wh_sb = const.tile([P, G4], BF16, name="wh_sb")
        nc.scalar.dma_start(out=wh_sb[:].rearrange("n (a k) -> n a k", a=4), in_=Wh.rearrange("a n k -> n a k"))
        brow = const.tile([P, G4], BF16, name="brow")
        nc.vector.memset(brow[:], 0.0)
        for i, b_in in enumerate((bx, bh)):
            nc.scalar.dma_start(out=brow[i:i + 1, :], in_=b_in.rearrange("(i a) n -> i (a n)", i=1))
        ones = const.tile([P, P], BF16, name="ones")
        nc.vector.memset(ones[:], 1.0)

        w_sb = const.tile([P, 4 * I], BF16, name="w_sb")
        xs = {}
        h_sb = {}
        c_sb = {}

        def load_x(q, lo, hi):
            if q not in xs:
                xs[q] = work.tile([P, 4 * I], BF16, tag="xs", bufs=XS_BUFS, name="xs")
            nc.sync.dma_start(out=xs[q][:, lo * I:hi * I], in_=x_v[:, (4 * q + lo) * I:(4 * q + hi) * I])

        def load_hc(ch, which, lo=0, hi=16):
            if which == "h":
                if ch not in h_sb:
                    h_sb[ch] = const.tile([P, 16 * H], BF16, name="h_sb%d" % ch)
                nc.sync.dma_start(out=h_sb[ch][:, lo * H:hi * H], in_=h_v[:, (ch * 16 + lo) * H:(ch * 16 + hi) * H])
            else:
                t = const.tile([P, 16 * H], BF16, name="c_sb%d" % ch)
                nc.sync.dma_start(out=t[:], in_=c_v[:, ch * 16 * H:(ch + 1) * 16 * H])
                c_sb[ch] = t

        for a in range(4):
            nc.sync.dma_start(out=w_sb[:, a * I:(a + 1) * I], in_=Wx[a])
        load_x(0, 0, 2)
        load_hc(0, "h", 0, 8)
        load_x(0, 2, 4)
        load_x(1, 0, 4)
        load_hc(0, "h", 8, 16)
        load_x(2, 0, 4)
        load_hc(0, "c")

        warm = const.tile([P, 1], F32, name="warm")
        nc.vector.memset(warm[:], 0.0)
        nc.scalar.activation(out=warm[:], in_=warm[:], func=AF.Sigmoid)

        ident_f = const.tile([P, P], F32, name="ident_f")
        make_identity(nc, ident_f[:])
        ident_b = const.tile([P, P], BF16, name="ident_b")
        make_identity(nc, ident_b[:])

        xts = {}
        grps = {}
        codes = {}
        scls = {}
        hTs = {}
        ghs = {}
        gxs = {}
        gxsb = {}
        gqs = {}
        t1s = {}
        t2s = {}
        cns = {}
        ths = {}

        w32 = w_sb[:].bitcast(F32)
        wgrp = const.tile([P, 2 * G4 * 4], BF16, name="wgrp", align_bytes=64)
        wgrp32 = wgrp[:].bitcast(F32).rearrange("p (g n u) -> p g n u", g=2, u=2)
        wc = const.tile([P, 2 * G4], U32, name="wc", align_bytes=64)
        ws = const.tile([P, 2 * G4], U8, name="ws", align_bytes=64)
        whT = const.tile([P, G4], BF16, name="whT")
        biasT = const.tile([P, 4], F32, name="biasT")
        bias_bc = const.tile([P, G4], F32, name="bias_bc")

        def prep_w(a, who):
            wt = psum.tile([P, 4, P], F32, tag="xt", bufs=XT_BUFS, name="wt")
            for gu in range(4):
                nc.tensor.transpose(wt[:, gu, :], w32[:, a * 512 + (gu // 2) * 256 + gu % 2:a * 512 + (gu // 2 + 1) * 256:2], ident_f[:])
            dst = wgrp32[:, :, POS[a] * P:(POS[a] + 1) * P, :]
            src = wt[:].rearrange("p (g u) n -> p g n u", g=2)
            if who == "s":
                nc.scalar.copy(out=dst, in_=src)
            else:
                nc.vector.tensor_copy(out=dst, in_=src)

        def quant_w():
            for g in range(2):
                nc.vector.quantize_mx(out=wc[:, g * G4:(g + 1) * G4].bitcast(FP8X4), scales=ws[:, g * G4:(g + 1) * G4],
                                      in_=wgrp[:, g * 4 * G4:(g + 1) * 4 * G4])

        def prep_wh():
            wht_ps = psum.tile([P, 4, P], BF16, tag="gx", bufs=GX_BUFS, name="wht_ps")
            for a in range(4):
                nc.tensor.transpose(wht_ps[:, POS[a], :], wh_sb[:, a * P:(a + 1) * P], ident_b[:])
            nc.vector.tensor_copy(out=whT[:], in_=wht_ps[:].rearrange("k a n -> k (a n)"))

        def prep_bias():
            bc_ps = psum.tile([P, 4, P], BF16, tag="ghc", bufs=2, name="bc_ps")
            for a in range(4):
                nc.tensor.transpose(bc_ps[:, a, :], brow[:, a * P:(a + 1) * P], ident_b[:])
            bc_sb = const.tile([P, 4, 2], F32, name="bc_sb")
            nc.vector.tensor_copy(out=bc_sb[:], in_=bc_ps[:, :, 0:2])
            b_ps = psum.tile([P, G4], F32, tag="ghc", bufs=2, name="b_ps")
            nc.tensor.matmul(b_ps[:], lhsT=ones[:], rhs=brow[:], start=True, stop=True)
            nc.vector.tensor_tensor(out=biasT[:], in0=bc_sb[:, :, 0], in1=bc_sb[:, :, 1], op=ALU.add)
            nc.vector.tensor_copy(out=bias_bc[:, 0:256], in_=b_ps[:, 0:256])
            nc.vector.tensor_copy(out=bias_bc[:, 256:384], in_=b_ps[:, 384:512])
            nc.vector.tensor_copy(out=bias_bc[:, 384:512], in_=b_ps[:, 256:384])

        def st_T(n):
            q, half = divmod(n, 2)
            x32 = xs[q][:].bitcast(F32)
            for jj in range(2):
                j4 = 2 * half + jj
                xt = psum.tile([P, 4, P], F32, tag="xt", bufs=XT_BUFS, name="xt")
                for gu in range(4):
                    nc.tensor.transpose(xt[:, gu, :], x32[:, j4 * 512 + (gu // 2) * 256 + gu % 2:j4 * 512 + (gu // 2 + 1) * 256:2], ident_f[:])
                xts[(n, jj)] = xt

        def st_XC(n, who):
            q, half = divmod(n, 2)
            if q not in grps:
                grps[q] = work.tile([P, 4096], BF16, tag="grp", bufs=GRP_BUFS, name="grp", align_bytes=64)
            g32 = grps[q][:].bitcast(F32).rearrange("p (f g j b u) -> p f g j b u", f=2, g=2, j=2, u=2)
            for jj in range(2):
                src = xts[(n, jj)][:].rearrange("p (g u) b -> p g b u", g=2)
                if who[jj] == "s":
                    nc.scalar.copy(out=g32[:, half, :, jj, :, :], in_=src)
                else:
                    nc.vector.tensor_copy(out=g32[:, half, :, jj, :, :], in_=src)

        def st_Q(q, lo, hi):
            if q not in codes:
                codes[q] = work.tile([P, 1024], U32, tag="codes", bufs=3, name="cd", align_bytes=64)
                scls[q] = work.tile([P, 1024], U8, tag="scl", bufs=3, name="sc", align_bytes=64)
            nc.vector.quantize_mx(out=codes[q][:, lo * 512:hi * 512].bitcast(FP8X4), scales=scls[q][:, lo * 512:hi * 512],
                                  in_=grps[q][:, lo * 2048:hi * 2048])

        def st_HT(o, who):
            hps = psum.tile([P, 8, P], BF16, tag="xt", bufs=XT_BUFS, name="hps")
            for k8 in range(8):
                ch, jc = divmod(8 * o + k8, 16)
                nc.tensor.transpose(hps[:, k8, :], h_sb[ch][:, jc * P:(jc + 1) * P], ident_b[:])
            hT = work.tile([P, 8 * P], BF16, tag="hT", bufs=3, name="hT")
            if who == "s":
                nc.scalar.copy(out=hT[:], in_=hps[:].rearrange("k j b -> k (j b)"))
            else:
                nc.vector.tensor_copy(out=hT[:], in_=hps[:].rearrange("k j b -> k (j b)"))
            hTs[o] = hT

        def gq_of(n):
            q = n // 2
            if q not in gqs:
                gqs[q] = work.tile([P, 4 * G4], F32, tag="gq", bufs=GQ_BUFS, name="gq")
            return gqs[q]

        def st_GHmm(n, jj):
            o, k8 = divmod(2 * n + jj, 8)
            if is_c(n) and n not in XT_C:
                gh = psum.tile([P, G4], F32, tag="ghc", bufs=2, name="ghc")
            else:
                gh = psum.tile([P, G4], F32, tag="xt", bufs=XT_BUFS, name="gha")
            nc.tensor.matmul(gh[:], lhsT=hTs[o][:, k8 * P:(k8 + 1) * P], rhs=whT[:], start=True, stop=not is_c(n))
            ghs[(n, jj)] = gh

        def st_GHadd(n, jj):
            for pos in range(4):
                nc.tensor.matmul(ghs[(n, jj)][:, pos * P:(pos + 1) * P],
                                 lhsT=gxsb[n][:, pos * 256 + jj * P:pos * 256 + (jj + 1) * P],
                                 rhs=ident_f[:], is_transpose=True, start=False, stop=(pos == 3))

        def st_GB(n, jj):
            gq = gq_of(n)
            j4 = 2 * (n % 2) + jj
            nc.vector.tensor_tensor(out=gq[:, j4 * G4:(j4 + 1) * G4], in0=ghs[(n, jj)][:], in1=bias_bc[:], op=ALU.add)

        def st_MX(n):
            q, half = divmod(n, 2)
            cd, sc = codes[q], scls[q]
            o0 = half * 512
            if is_c(n):
                for bk in range(2):
                    gx = psum.tile([P, G4], F32, tag="gx", bufs=GX_BUFS, name="gx")
                    for hf in range(2):
                        pos = 2 * bk + hf
                        for g in range(2):
                            wsl = slice(g * G4 + pos * P, g * G4 + (pos + 1) * P)
                            xsl = slice(o0 + g * 256, o0 + (g + 1) * 256)
                            nc.tensor.matmul_mx(out=gx[:, hf * 256:(hf + 1) * 256],
                                                lhsT=wc[:, wsl].bitcast(FP8X4), lhsT_scale=ws[:, wsl],
                                                rhs=cd[:, xsl].bitcast(FP8X4), rhs_scale=sc[:, xsl],
                                                start=(g == 0), stop=(g == 1))
                    gxs[(n, bk)] = gx
            else:
                for jj in range(2):
                    gx = psum.tile([P, G4], F32, tag="gx", bufs=GX_BUFS, name="gx")
                    for g in range(2):
                        xsl = slice(o0 + (2 * g + jj) * P, o0 + (2 * g + jj + 1) * P)
                        wsl = slice(g * G4, (g + 1) * G4)
                        nc.tensor.matmul_mx(out=gx[:], lhsT=cd[:, xsl].bitcast(FP8X4), lhsT_scale=sc[:, xsl],
                                            rhs=wc[:, wsl].bitcast(FP8X4), rhs_scale=ws[:, wsl],
                                            start=(g == 0), stop=(g == 1))
                    gxs[(n, jj)] = gx

        def st_AD(n, jj):
            gq = gq_of(n)
            j4 = 2 * (n % 2) + jj
            sl = gq[:, j4 * G4:(j4 + 1) * G4]
            nc.vector.tensor_tensor(out=sl, in0=gxs[(n, jj)][:], in1=sl, op=ALU.add)

        def st_CP(n, bk, who):
            if n not in gxsb:
                gxsb[n] = work.tile([P, 4 * 256], F32, tag="gxsb", bufs=2, name="gxsb")
            t = gxsb[n]
            for hf in range(2):
                pos = 2 * bk + hf
                a = INV[pos]
                if who == "v":
                    nc.vector.tensor_scalar_add(out=t[:, pos * 256:(pos + 1) * 256],
                                                in0=gxs[(n, bk)][:, hf * 256:(hf + 1) * 256], scalar1=biasT[:, a:a + 1])
                else:
                    nc.scalar.activation(out=t[:, pos * 256:(pos + 1) * 256],
                                         in_=gxs[(n, bk)][:, hf * 256:(hf + 1) * 256], func=AF.Identity,
                                         bias=biasT[:, a:a + 1])

        def st_ACT(n, tiles=(0, 1)):
            gq = gq_of(n)
            if is_c(n):
                for jj in tiles:
                    j4 = 2 * (n % 2) + jj
                    nc.scalar.activation(out=gq[:, j4 * G4:j4 * G4 + 384], in_=ghs[(n, jj)][:, 0:384], func=AF.Sigmoid)
                    nc.scalar.activation(out=gq[:, j4 * G4 + 384:(j4 + 1) * G4], in_=ghs[(n, jj)][:, 384:512], func=AF.Tanh)
            else:
                g3 = gq[:].rearrange("p (j n) -> p j n", j=4)
                j0 = 2 * (n % 2)
                nc.scalar.activation(out=g3[:, j0:j0 + 2, 0:384], in_=g3[:, j0:j0 + 2, 0:384], func=AF.Sigmoid)
                nc.scalar.activation(out=g3[:, j0:j0 + 2, 384:512], in_=g3[:, j0:j0 + 2, 384:512], func=AF.Tanh)

        def gview(u):
            q, j0, nj = u
            return gqs[q][:].rearrange("p (j n) -> p j n", j=4)[:, j0:j0 + nj, :]

        def v3(t, u):
            return t[:, 0:u[2] * H].rearrange("p (j n) -> p j n", j=u[2])

        def st_t1(u, e):
            q, j0, nj = u
            ch, q4 = divmod(q, 4)
            c3 = c_sb[ch][:, q4 * 512 + j0 * H:q4 * 512 + (j0 + nj) * H].rearrange("p (j n) -> p j n", j=nj)
            t1s[u] = work.tile([P, nj * H], F32, tag="t1_%d" % nj, bufs=(T1_BUFS if nj == 4 else 2), name="t1")
            eng[e].tensor_tensor(out=v3(t1s[u], u), in0=gview(u)[:, :, 128:256], in1=c3, op=ALU.mult)

        def st_t2(u, e):
            t2s[u] = work.tile([P, u[2] * H], F32, tag="t2_%d" % u[2], bufs=(T2_BUFS if u[2] == 4 else 2), name="t2")
            eng[e].tensor_tensor(out=v3(t2s[u], u), in0=gview(u)[:, :, 0:128], in1=gview(u)[:, :, 384:512], op=ALU.mult)

        def st_cn(u, e):
            q, j0, nj = u
            w = nj * H
            cn = work.tile([P, 512], F32, tag="cn", bufs=5, name="cn")
            eng[e].tensor_tensor(out=cn[:, 0:w], in0=t1s[u][:, 0:w], in1=t2s[u][:, 0:w], op=ALU.add)
            nc.sync.dma_start(out=cn_v[:, q * 512 + j0 * H:q * 512 + (j0 + nj) * H], in_=cn[:, 0:w])
            cns[u] = cn

        def st_TC(u):
            w = u[2] * H
            th = work.tile([P, 512], F32, tag="th", bufs=2, name="th")
            nc.scalar.activation(out=th[:, 0:w], in_=cns[u][:, 0:w], func=AF.Tanh)
            ths[u] = th

        def st_hs(u, e):
            q, j0, nj = u
            w = nj * H
            hs = work.tile([P, 512], F32, tag="hs", bufs=5, name="hs")
            eng[e].tensor_tensor(out=v3(hs, u), in0=gview(u)[:, :, 256:384], in1=v3(ths[u], u), op=ALU.mult)
            nc.sync.dma_start(out=hs_v[:, q * 512 + j0 * H:q * 512 + (j0 + nj) * H], in_=hs[:, 0:w])

        prep_wh()
        prep_w(0, "s")
        prep_w(1, "v")
        prep_w(2, "s")
        prep_w(3, "v")
        st_T(0)
        st_XC(0, "ss")
        quant_w()
        st_Q(0, 0, 1)
        st_HT(0, "s")
        prep_bias()
        st_T(1)
        st_XC(1, "sv")

        def quad(q):
            return (q, 0, 4)

        def pair(n):
            return (n // 2, 2 * (n % 2), 2)

        def tmax(m):
            return min(m + LOOK, 2 * m + 1, NPAIR - 1)

        NSTEADY = NQUAD - 2

        def hs_eng(q):
            if q >= NSTEADY - 1 or HS_ENG == "v":
                return "v"
            if HS_ENG == "g":
                return "g"
            return "g" if q % 2 == int(HS_ENG) else "v"

        for m in range(NPAIR):
            p2 = m - 2
            if p2 >= 0 and is_c(p2):
                st_GHadd(p2, 0)
                st_GHadd(p2, 1)
                st_ACT(p2)
            if m > 0:
                for n in range(tmax(m - 1) + 1, tmax(m) + 1):
                    if n % 2 == 0 and 3 <= n // 2 + 2 < NQUAD:
                        load_x(n // 2 + 2, 0, 4)
                    if n % 8 == 2 and n // 8 + 1 < 4:
                        load_hc(n // 8 + 1, "h")
                        load_hc(n // 8 + 1, "c")
                    st_T(n)
                    st_XC(n, (XCE if n % 2 == 0 else XCO) if n >= 6 else "sv")
                    if (n + 2) % 4 == 0 and (n + 2) // 4 < 8:
                        st_HT((n + 2) // 4, HTE)
            if p2 >= 0 and not is_c(p2):
                st_ACT(p2)
            st_GHmm(m, 0)
            if not is_c(m):
                st_GB(m, 0)
            if m == 0:
                st_Q(0, 1, 2)
            if m % 2 == 1:
                if (m + 1) // 2 < NQUAD:
                    st_Q((m + 1) // 2, 0, 2)
                q = (m - 5) // 2
                if 0 <= q - 1 < NSTEADY and hs_eng(q - 1) == "v":
                    st_hs(quad(q - 1), "v")
                if 0 <= q < NSTEADY:
                    st_cn(quad(q), "v")
                if 0 <= q + 1 < NSTEADY:
                    st_t1(quad(q + 1), "g" if q + 1 < NSTEADY - 1 else "v")
                    st_t2(quad(q + 1), "g" if q + 1 < NSTEADY - 1 else "v")
                if 0 <= q < NSTEADY and hs_eng(q) == "g":
                    st_TC(quad(q))
                    st_hs(quad(q), "g")
            st_MX(m)
            st_GHmm(m, 1)
            if is_c(m):
                st_CP(m, 0, CP0 if (m // 2) % 2 == 0 else CP0B)
                st_CP(m, 1, "s" if m >= NPAIR - TAIL_S else (CP1 if (m // 2) % 2 == 0 else CP1B))
            else:
                st_AD(m, 0)
                st_GB(m, 1)
                st_AD(m, 1)
            if m % 2 == 1 and 0 <= (m - 5) // 2 < NSTEADY and hs_eng((m - 5) // 2) == "v":
                st_TC(quad((m - 5) // 2))

        last = NPAIR - 1
        q14 = quad(NQUAD - 2)
        ta, tb = (NQUAD - 1, 2, 1), (NQUAD - 1, 3, 1)
        p30 = pair(last - 1)
        st_GHadd(30, 0)
        st_GHadd(30, 1)
        st_ACT(30)
        st_t1(q14, "v")
        st_t2(q14, "v")
        st_hs(quad(NQUAD - 3), "v")
        st_cn(q14, "v")
        st_GHadd(31, 0)
        st_GHadd(31, 1)
        st_ACT(31, (0,))
        st_TC(q14)
        st_t1(p30, "v")
        st_t2(p30, "v")
        st_ACT(31, (1,))
        st_cn(p30, "v")
        st_t1(ta, "v")
        st_TC(p30)
        st_t2(ta, "v")
        st_hs(q14, "v")
        st_cn(ta, "v")
        st_t1(tb, "v")
        st_TC(ta)
        st_t2(tb, "v")
        st_hs(p30, "v")
        st_cn(tb, "v")
        st_TC(tb)
        st_hs(ta, "v")
        st_hs(tb, "v")
